import numpy as np
import ml_dtypes


def mxq(x, axis, fmt="e4m3"):
    dtype, down = {"e4m3": (ml_dtypes.float8_e4m3fn, 7), "e5m2": (ml_dtypes.float8_e5m2, 14)}[fmt]
    v = np.moveaxis(np.asarray(x, np.float32).astype(ml_dtypes.bfloat16).astype(np.float64), axis, -1)
    blocks = v.reshape(v.shape[:-1] + (-1, 32))
    amax = np.abs(blocks).max(-1, keepdims=True)
    byte = np.maximum(np.where(amax > 0, np.frexp(amax)[1] - 1 + 127, 0) - down, 1)
    scale = np.exp2(byte - 127.0)
    codes = (blocks / scale).astype(np.float32).astype(dtype).astype(np.float64)
    return np.moveaxis((codes * scale).reshape(v.shape), -1, axis)


WIDE = False


def mx_kscale(k):
    if not WIDE:
        return np.ones(k)
    levels = np.array([10, -10, 5, -5, 0])
    if k % 512:
        return np.exp2(np.random.permutation(np.resize(levels, k // 32))).repeat(32)
    a = np.empty((k // 512, 16))
    for p in range(k // 512):
        a[p, :8] = np.random.permutation(np.resize(levels, 8))
        for g in range(8):
            far = levels[np.abs(levels - a[p, g]) >= 10]
            a[p, g + 8] = far[np.random.randint(len(far))]
    return np.exp2(a.ravel()).repeat(32)


BF16 = ml_dtypes.bfloat16


def bf(x):
    return np.asarray(x, np.float32).astype(BF16)


def f64(x):
    return np.asarray(x).astype(np.float64)


B, T, C = 8, 512, 512
EPS = 1e-8


def sigmoid(z):
    return 1.0 / (1.0 + np.exp(-z))


def setup_inputs():
    s = mx_kscale(C)
    t = mx_kscale(C)
    g = 1.0 / np.sqrt(C)
    return {
        "x": bf(np.random.standard_normal((B, T, C)) * s),
        "a0": bf(np.random.standard_normal((B, C)) * t),
        "b0": bf(0.5 + np.random.uniform(size=(B, C))),
        "x_prev0": bf(np.random.standard_normal((B, C)) * s),
        "w": bf((0.5 + 2.0 * np.random.uniform(size=C)) / T),
        "u": bf(np.random.standard_normal(C) * 0.5),
        "mu_r": bf(np.random.uniform(size=C)),
        "mu_k": bf(np.random.uniform(size=C)),
        "mu_v": bf(np.random.uniform(size=C)),
        "W_r": bf(np.random.standard_normal((C, C)) * g / s[None, :]),
        "W_k": bf(np.random.standard_normal((C, C)) * g / s[None, :]),
        "W_v": bf(np.random.standard_normal((C, C)) * g / s[None, :] * t[:, None]),
        "W_out": bf(np.random.standard_normal((C, C)) * 2.0 * g / t[None, :]),
    }


def reference(x, a0, b0, x_prev0, w, u, mu_r, mu_k, mu_v, W_r, W_k, W_v, W_out):
    x, a0, b0, x_prev0 = f64(x), f64(a0), f64(b0), f64(x_prev0)
    w, u = f64(w), f64(u)
    mu_r, mu_k, mu_v = f64(mu_r), f64(mu_k), f64(mu_v)
    x_shift = np.concatenate([x_prev0[:, None, :], x[:, :-1, :]], axis=1)
    xr = mu_r * x + (1.0 - mu_r) * x_shift
    xk = mu_k * x + (1.0 - mu_k) * x_shift
    xv = mu_v * x + (1.0 - mu_v) * x_shift
    r = sigmoid(mxq(xr, 2, "e4m3") @ mxq(f64(W_r), 1, "e4m3").T)
    k = mxq(xk, 2, "e4m3") @ mxq(f64(W_k), 1, "e4m3").T
    v = mxq(xv, 2, "e4m3") @ mxq(f64(W_v), 1, "e4m3").T
    ek = np.exp(u + k)
    steps = np.arange(1, T + 1).astype(np.float64)
    decay_pow = np.exp(-w[None, :] * steps[:, None])
    a_t = a0[:, None, :] * decay_pow[None]
    b_t = b0[:, None, :] * decay_pow[None]
    wkv = (a_t + ek * v) / (b_t + ek + EPS)
    h = r * wkv
    return mxq(h, 2, "e4m3") @ mxq(f64(W_out), 1, "e4m3").T

@@ -1,0 +1,541 @@
+from contextlib import ExitStack
+
+import concourse.masks as masks
+import concourse.mybir as mybir
+
+FP8X4 = mybir.dt.float8_e4m3fn_x4
+BF16 = mybir.dt.bfloat16
+F32 = mybir.dt.float32
+I32 = mybir.dt.int32
+U32 = mybir.dt.uint32
+U8 = mybir.dt.uint8
+ALU = mybir.AluOpType
+AF = mybir.ActivationFunctionType
+
+P = 128
+B = 8
+T = 512
+C = 512
+J = 4
+EPS = 1e-8
+PADC = 16
+FLOPS = 4 * 2 * B * T * C * C
+MANUAL = True
+QPOS = (10, 11, 12, 12)
+NH = 4
+
+
+def tile_rwkv_timemix_pa_t_kernel(
+    tc, x, a0, b0, x_prev0, w, u, mu_r, mu_k, mu_v, W_r, W_k, W_v, W_out, out
+):
+    nc = tc.nc
+    with ExitStack() as ctx:
+        if MANUAL:
+            ctx.enter_context(tc.manual_schedule())
+        const = ctx.enter_context(tc.tile_pool(name="const", bufs=1))
+        work = ctx.enter_context(tc.tile_pool(name="work", bufs=2))
+        psum = ctx.enter_context(tc.psum_pool(name="psum", bufs=8))
+
+        def bank(shape, dtype, name):
+            return psum.tile(shape, dtype, name=name, tag="ps", bufs=8)
+
+        prma = const.tile([P, C], BF16)
+        prmb = const.tile([P, C], BF16)
+        nc.vector.memset(prma[:], 0.0)
+        nc.vector.memset(prmb[:], 0.0)
+        nc.sync.dma_start(
+            out=prma[32:64, :], in_=x.rearrange("b (i t) c -> (b i) t c", t=P)[:, P - 1, :]
+        )
+        for r, vec in enumerate((mu_r, mu_k, mu_v)):
+            nc.scalar.dma_start(out=prma[r : r + 1, :], in_=vec.rearrange("(o c) -> o c", o=1))
+        nc.scalar.dma_start(out=prma[24:32, :], in_=x_prev0)
+        for r, vec in enumerate((w, u)):
+            nc.scalar.dma_start(out=prmb[r : r + 1, :], in_=vec.rearrange("(o c) -> o c", o=1))
+        nc.scalar.dma_start(out=prmb[8:16, :], in_=a0)
+        nc.scalar.dma_start(out=prmb[16:24, :], in_=b0)
+
+        xn = {}
+
+        def load_x(b, queue):
+            xn[b] = work.tile([P, 4, C], BF16, name="xn", tag="xn", bufs=3)
+            queue.dma_start(out=xn[b][:], in_=x[b].rearrange("(i p) c -> p i c", p=P))
+
+        wnat = {}
+
+        def load_w(key, wap):
+            wnat[key] = const.tile([P, 4, C], BF16, name="wn" + key, tag="wn" + key)
+            rows = "(a p) c -> p a c" if key == "o" else "(p a) c -> p a c"
+            nc.scalar.dma_start(out=wnat[key][:], in_=wap.rearrange(rows, p=P))
+
+        xn[0] = work.tile([P, 4, C], BF16, name="xn", tag="xn", bufs=3)
+        for hh in range(2):
+            nc.sync.dma_start(
+                out=xn[0][:, :, hh * 256 : (hh + 1) * 256],
+                in_=x[0, :, hh * 256 : (hh + 1) * 256].rearrange("(i p) c -> p i c", p=P),
+            )
+
+        ident = const.tile([P, P], BF16)
+        masks.make_identity(nc, ident[:])
+        it_i = const.tile([P, T], I32)
+        nc.gpsimd.iota(it_i[:], pattern=[[1, T]], base=1, channel_multiplier=0)
+        half = const.tile([P, 1], F32)
+        nc.vector.memset(half[:], 0.5)
+        dummy = const.tile([P, 1], F32)
+        nc.scalar.activation(out=dummy[:], in_=half[:], func=AF.Ln)
+        load_w("k", W_k)
+        load_w("r", W_r)
+        load_w("v", W_v)
+        load_x(1, nc.scalar)
+        load_w("o", W_out)
+        load_x(2, nc.scalar)
+        dmat = const.tile([P, P], BF16)
+        nc.vector.tensor_copy(out=dmat[:, 0:1], in_=ident[:, 0:1])
+        nc.vector.tensor_tensor(
+            out=dmat[:, 1:P], in0=ident[:, 1:P], in1=ident[:, 0 : P - 1], op=ALU.subtract
+        )
+        sel = const.tile([P, B, 4, 8], BF16)
+        nc.vector.memset(sel[:], 0.0)
+        nc.vector.tensor_scalar(
+            out=sel[:, :, 0, 0], in0=ident[:, 24:32], scalar1=-1.0, scalar2=None, op0=ALU.mult
+        )
+        nc.vector.tensor_scalar(
+            out=sel[:, :, 1:4, 0],
+            in0=ident[:, 32:64].rearrange("p (b i) -> p b i", i=4)[:, :, 0:3],
+            scalar1=-1.0,
+            scalar2=None,
+            op0=ALU.mult,
+        )
+        it_f = const.tile([P, T], F32)
+        nc.vector.tensor_copy(out=it_f[:], in_=it_i[:])
+
+        xT = {}
+        dd = {}
+        xtp = {}
+
+        def make_dd(b, j):
+            t = bank([P, T], F32, "dd")
+            dd[(b, j)] = t
+            for i in range(4):
+                nc.tensor.matmul(
+                    out=t[:, i * P : (i + 1) * P],
+                    lhsT=xn[b][:, i, j:C:J],
+                    rhs=dmat[:],
+                    start=(i == 0),
+                    stop=False,
+                )
+            nc.tensor.matmul(
+                out=t[:].rearrange("p (i e) -> p i e", e=P)[:, :, 0:8],
+                lhsT=prma[:, j:C:J],
+                rhs=sel[:, b, :, :],
+                start=False,
+                stop=True,
+            )
+
+        def transposes(b, halves):
+            for jh in halves:
+                xt = bank([P, 2, T], BF16, "xt")
+                xtp[(b, jh)] = xt
+                for jj in range(2):
+                    j = 2 * jh + jj
+                    for i in range(4):
+                        nc.tensor.transpose(
+                            out=xt[:, jj, i * P : (i + 1) * P],
+                            in_=xn[b][:, i, j:C:J],
+                            identity=ident[:],
+                        )
+
+        def evac_xT(b):
+            xT[b] = work.tile([P, J, PADC + T], BF16, name="xT", tag="xT", bufs=2)
+            nc.gpsimd.tensor_copy(out=xT[b][:, :, PADC - 1 : PADC], in_=xpT[:, :, b : b + 1])
+            for jh in range(2):
+                nc.scalar.copy(out=xT[b][:, 2 * jh : 2 * jh + 2, PADC:], in_=xtp[(b, jh)][:])
+
+        wc = {}
+        ws = {}
+        wg = {}
+
+        def prep_w(key):
+            wg[key] = const.tile([P, C, J], BF16, name="wg", tag="wg", bufs=3, align_bytes=64)
+            for h in range(2):
+                wt = bank([P, 2, J, P], BF16, "wt")
+                for a in range(2):
+                    for j in range(J):
+                        nc.tensor.transpose(
+                            out=wt[:, a, j, :],
+                            in_=wnat[key][:, 2 * h + a, j:C:J],
+                            identity=ident[:],
+                        )
+                nc.scalar.copy(
+                    out=wg[key][:, 256 * h : 256 * h + 256, :].rearrange("p (a o) j -> p a o j", a=2),
+                    in_=wt[:].rearrange("p a j o -> p a o j"),
+                )
+
+        def quant_w(key):
+            wc[key] = const.tile([P, C], U32, name="wc" + key, tag="wc" + key, align_bytes=64)
+            ws[key] = const.tile([P, C], U8, name="ws" + key, tag="ws" + key, align_bytes=64)
+            nc.vector.quantize_mx(
+                out=wc[key][:].bitcast(FP8X4),
+                scales=ws[key][:],
+                in_=wg[key][:].rearrange("p o j -> p (o j)"),
+            )
+
+        pl = {}
+        gr = {}
+        xc = {}
+        xs = {}
+        MS = ("r", "k", "v")
+
+        def mix(b, j, mi):
+            m = MS[mi]
+            if j == 0:
+                pl[m] = work.tile([P, J, T], BF16, name="pl" + m, tag="pl" + m, bufs=1)
+            nc.vector.scalar_tensor_tensor(
+                out=pl[m][:, j, :],
+                in0=dd[(b, j)][:],
+                scalar=pfa[:, j, mi : mi + 1],
+                in1=xT[b][:, j, PADC - 1 : PADC - 1 + T],
+                op0=ALU.mult,
+                op1=ALU.add,
+            )
+
+        def regroup(b, m, on_pool):
+            gr[m] = work.tile([P, T, J], BF16, name="gr", tag="gr", bufs=3, align_bytes=64)
+            if on_pool:
+                nc.gpsimd.tensor_scalar(
+                    out=gr[m][:],
+                    in0=pl[m][:].rearrange("p t w -> p w t"),
+                    scalar1=1.0,
+                    scalar2=0.0,
+                    op0=ALU.mult,
+                    op1=ALU.add,
+                )
+            else:
+                nc.vector.tensor_copy(
+                    out=gr[m][:].rearrange("p (c i) t -> p c t i", i=4),
+                    in_=pl[m][:].rearrange("p t (c i) -> p c t i", i=4),
+                )
+
+        def quant_x(b, m):
+            xc[(b, m)] = work.tile([P, T], U32, name="xc" + m, tag="xc" + m, bufs=2, align_bytes=64)
+            xs[(b, m)] = work.tile([P, T], U8, name="xs" + m, tag="xs" + m, bufs=2, align_bytes=64)
+            nc.vector.quantize_mx(
+                out=xc[(b, m)][:].bitcast(FP8X4),
+                scales=xs[(b, m)][:],
+                in_=gr[m][:].rearrange("p w t -> p (w t)"),
+            )
+
+        ee = {}
+        th = {}
+        qq = {}
+        dn = {}
+        ps = {}
+
+        def alloc_b(b):
+            ee[b] = work.tile([P, J, T], F32, name="ee", tag="ee", bufs=2)
+            th[b] = work.tile([P, J, T], F32, name="th", tag="th", bufs=2)
+            qq[b] = work.tile([P, J, T], F32, name="qq", tag="qq", bufs=2)
+            dn[b] = work.tile([P, J, T], F32, name="dn", tag="dn", bufs=2)
+
+        def s1_mm(b, j, m):
+            ps[(b, j, m)] = bank([P, T], F32, "s1" + m)
+            nc.tensor.matmul_mx(
+                out=ps[(b, j, m)][:],
+                lhsT=wc[m][:, j * P : (j + 1) * P].bitcast(FP8X4),
+                lhsT_scale=ws[m][:, j * P : (j + 1) * P],
+                rhs=xc[(b, m)][:].bitcast(FP8X4),
+                rhs_scale=xs[(b, m)][:],
+                start=True,
+                stop=True,
+            )
+
+        def e_exp(b, j):
+            nc.scalar.activation(
+                out=ee[b][:, j, :], in_=ps[(b, j, "k")][:], func=AF.Exp, bias=beta[:, j, b : b + 1]
+            )
+
+        def e_tanh(b, j):
+            nc.scalar.activation(out=th[b][:, j, :], in_=ps[(b, j, "r")][:], func=AF.Tanh, scale=0.5)
+
+        def den(b, j, eng):
+            eng.tensor_tensor(out=dn[b][:, j, :], in0=ee[b][:, j, :], in1=dtab[:, j, :], op=ALU.add)
+
+        def d_q(b, j):
+            nc.vector.scalar_tensor_tensor(
+                out=qq[b][:, j, :],
+                in0=ps[(b, j, "v")][:],
+                scalar=g0[:, j, b : b + 1],
+                in1=ee[b][:, j, :],
+                op0=ALU.subtract,
+                op1=ALU.mult,
+            )
+
+        def a_ln(b, j):
+            nc.scalar.activation(
+                out=dn[b][:, j, :], in_=dn[b][:, j, :], func=AF.Ln, bias=et[:, j, b : b + 1]
+            )
+
+        def a_rho(b):
+            nc.scalar.activation(out=dn[b][:], in_=dn[b][:], func=AF.Exp, scale=-1.0)
+
+        def a_rhoj(b, j):
+            nc.scalar.activation(out=dn[b][:, j, :], in_=dn[b][:, j, :], func=AF.Exp, scale=-1.0)
+
+        def d_x(b, j):
+            nc.vector.scalar_tensor_tensor(
+                out=qq[b][:, j, :],
+                in0=qq[b][:, j, :],
+                scalar=g0e[:, j, b : b + 1],
+                in1=dn[b][:, j, :],
+                op0=ALU.subtract,
+                op1=ALU.mult,
+            )
+
+        def y_act(b, j):
+            nc.scalar.activation(
+                out=qq[b][:, j, :],
+                in_=qq[b][:, j, :],
+                func=AF.Identity,
+                scale=0.5,
+                bias=g0h[:, j, b : b + 1],
+            )
+
+        def y_dve(b, j):
+            nc.vector.tensor_scalar(
+                out=qq[b][:, j, :],
+                in0=qq[b][:, j, :],
+                scalar1=half[:, 0:1],
+                scalar2=g0h[:, j, b : b + 1],
+                op0=ALU.mult,
+                op1=ALU.add,
+            )
+
+        hg = {}
+        hc = {}
+        hs = {}
+
+        def gate(b, h, nh):
+            if h == 0:
+                hg[b] = work.tile([P, T, J], BF16, name="hg", tag="hg", bufs=2, align_bytes=64)
+            n = T // nh
+            nc.vector.scalar_tensor_tensor(
+                out=hg[b][:, h * n : (h + 1) * n, :],
+                in0=th[b][:, :, h * n : (h + 1) * n].rearrange("p j t -> p t j"),
+                scalar=1.0,
+                in1=qq[b][:, :, h * n : (h + 1) * n].rearrange("p j t -> p t j"),
+                op0=ALU.add,
+                op1=ALU.mult,
+            )
+
+        def quant_h(b, h, nh):
+            if h == 0:
+                hc[b] = work.tile([P, T], U32, name="hc", tag="hc", bufs=2, align_bytes=64)
+                hs[b] = work.tile([P, T], U8, name="hs", tag="hs", bufs=2, align_bytes=64)
+            n = T // nh
+            nc.vector.quantize_mx(
+                out=hc[b][:, h * n : (h + 1) * n].bitcast(FP8X4),
+                scales=hs[b][:, h * n : (h + 1) * n],
+                in_=hg[b][:, h * n : (h + 1) * n, :].rearrange("p w t -> p (w t)"),
+            )
+
+        po = {}
+        ost = {}
+
+        def s2_mm(b, i):
+            po[(b, i)] = bank([P, C], F32, "po")
+            nc.tensor.matmul_mx(
+                out=po[(b, i)][:],
+                lhsT=hc[b][:, i * P : (i + 1) * P].bitcast(FP8X4),
+                lhsT_scale=hs[b][:, i * P : (i + 1) * P],
+                rhs=wc["o"][:].bitcast(FP8X4),
+                rhs_scale=ws["o"][:],
+                start=True,
+                stop=True,
+            )
+
+        def ao(b, i, on_vector):
+            if i == 0:
+                ost[b] = work.tile([P, 4, C], F32, name="ost", tag="ost", bufs=2)
+            if on_vector:
+                nc.vector.tensor_copy(out=ost[b][:, i, :], in_=po[(b, i)][:])
+            else:
+                nc.scalar.copy(out=ost[b][:, i, :], in_=po[(b, i)][:])
+
+        def store(b, h, nh):
+            n = 4 // nh
+            nc.sync.dma_start(
+                out=out[b, h * n * P : (h + 1) * n * P, :].rearrange("(i p) c -> p i c", p=P),
+                in_=ost[b][:, h * n : (h + 1) * n, :],
+            )
+
+        pta = bank([P, J, P], BF16, "pta")
+        for j in range(J):
+            nc.tensor.transpose(out=pta[:, j, :], in_=prma[:, j:C:J], identity=ident[:])
+        pfa = const.tile([P, J, 4], F32)
+        nc.vector.tensor_copy(out=pfa[:], in_=pta[:, :, 0:4])
+        xpT = const.tile([P, J, B], BF16)
+        nc.vector.tensor_copy(out=xpT[:], in_=pta[:, :, 24:32])
+        transposes(0, (0,))
+        make_dd(0, 0)
+        make_dd(0, 1)
+        transposes(0, (1,))
+        make_dd(0, 2)
+        make_dd(0, 3)
+        evac_xT(0)
+        ptb = bank([P, J, P], BF16, "ptb")
+        for j in range(J):
+            nc.tensor.transpose(out=ptb[:, j, :], in_=prmb[:, j:C:J], identity=ident[:])
+        pfb = const.tile([P, J, 24], F32)
+        nc.vector.tensor_copy(out=pfb[:], in_=ptb[:, :, 0:24])
+        negw = const.tile([P, J], F32)
+        nc.vector.tensor_scalar(out=negw[:], in0=pfb[:, :, 0], scalar1=-1.0, scalar2=None, op0=ALU.mult)
+        rb0 = const.tile([P, J, B], F32)
+        nc.vector.reciprocal(out=rb0[:], in_=pfb[:, :, 16:24])
+        g0 = const.tile([P, J, B], F32)
+        nc.vector.tensor_tensor(out=g0[:], in0=pfb[:, :, 8:16], in1=rb0[:], op=ALU.mult)
+        et = const.tile([P, J, B], F32)
+        nc.vector.tensor_scalar(out=et[:], in0=rb0[:], scalar1=EPS, scalar2=None, op0=ALU.mult)
+        g0e = const.tile([P, J, B], F32)
+        nc.vector.tensor_tensor(out=g0e[:], in0=g0[:], in1=et[:], op=ALU.mult)
+        g0h = const.tile([P, J, B], F32)
+        nc.vector.tensor_scalar(out=g0h[:], in0=g0[:], scalar1=0.5, scalar2=None, op0=ALU.mult)
+        lnb = const.tile([P, J, B], F32)
+        nc.scalar.activation(out=lnb[:], in_=pfb[:, :, 16:24], func=AF.Ln)
+        dtab = const.tile([P, J, T], F32)
+        beta = const.tile([P, J, B], F32)
+
+        for m in range(B):
+            has_n = m + 1 < B
+            h1 = m >= 1
+            h2 = m >= 2
+            h3 = m >= 3
+            if h1 and m + 2 < B:
+                load_x(m + 2, nc.sync)
+            if h1:
+                alloc_b(m - 1)
+                for j in range(J):
+                    s1_mm(m - 1, j, "k")
+                for j in range(J):
+                    e_exp(m - 1, j)
+                    if m == 1:
+                        nc.scalar.activation(
+                            out=dtab[:, j, :], in_=it_f[:], func=AF.Exp, scale=negw[:, j : j + 1]
+                        )
+                    den(m - 1, j, nc.gpsimd)
+                    s1_mm(m - 1, j, "r")
+                for j in range(J):
+                    e_tanh(m - 1, j)
+                    s1_mm(m - 1, j, "v")
+            qd = 0
+            for s in range(13):
+                while h1 and qd < J and QPOS[qd] <= s:
+                    d_q(m - 1, qd)
+                    qd += 1
+                if s < 12:
+                    mix(m, s % 4, (1, 0, 2)[s // 4])
+                    if s >= 8 and has_n:
+                        make_dd(m + 1, s % 4)
+                    if s == 3:
+                        regroup(m, "k", True)
+                    if s == 7 and m == 0:
+                        regroup(m, "r", True)
+                if m == 0 and s == 2:
+                    prep_w("k")
+                    transposes(1, (0, 1))
+                    evac_xT(1)
+                    prep_w("r")
+                if m == 0 and s == 8:
+                    prep_w("v")
+            if h1:
+                for j in range(J):
+                    a_ln(m - 1, j)
+            if h3:
+                for i in range(4):
+                    s2_mm(m - 3, i)
+                    ao(m - 3, i, False)
+                store(m - 3, 0, 1)
+            if m == 1:
+                prep_w("o")
+            if h2:
+                for j in range(J):
+                    d_x(m - 2, j)
+                for j in range(J):
+                    y_act(m - 2, j)
+            if h1 and has_n:
+                transposes(m + 1, (0, 1))
+                evac_xT(m + 1)
+            if h1:
+                a_rho(m - 1)
+            if m == 0:
+                nc.vector.tensor_tensor(
+                    out=beta[:], in0=pfb[:, :, 1:2].to_broadcast([P, J, B]), in1=lnb[:], op=ALU.subtract
+                )
+            if m > 0:
+                regroup(m, "r", False)
+            regroup(m, "v", False)
+            if m == 0:
+                quant_w("k")
+            quant_x(m, "k")
+            if h2:
+                gate(m - 2, 0, 1)
+            if m == 0:
+                quant_w("r")
+            quant_x(m, "r")
+            if m == 0:
+                quant_w("v")
+            if m == 1:
+                quant_w("o")
+            quant_x(m, "v")
+            if h2:
+                quant_h(m - 2, 0, 1)
+
+        l7 = B - 1
+        l6 = B - 2
+        l5 = B - 3
+        alloc_b(l7)
+        for j in range(J):
+            s1_mm(l7, j, "k")
+        for j in range(J):
+            e_exp(l7, j)
+            den(l7, j, nc.vector)
+        for j in range(J):
+            s1_mm(l7, j, "v")
+        for j in range(J):
+            d_q(l7, j)
+        for j in range(J):
+            a_ln(l7, j)
+        for j in range(J):
+            d_x(l6, j)
+        for j in range(J):
+            y_dve(l6, j)
+        for j in range(J):
+            a_rhoj(l7, j)
+        for j in range(J):
+            s1_mm(l7, j, "r")
+        for j in range(J):
+            e_tanh(l7, j)
+        for i in range(4):
+            s2_mm(l5, i)
+            ao(l5, i, False)
+        store(l5, 0, 1)
+        gate(l6, 0, 1)
+        d_x(l7, 0)
+        d_x(l7, 1)
+        quant_h(l6, 0, 1)
+        d_x(l7, 2)
+        d_x(l7, 3)
+        for j in range(J):
+            y_dve(l7, j)
+        for i in range(4):
+            s2_mm(l6, i)
+            ao(l6, i, False)
+        store(l6, 0, 1)
+        for h in range(NH):
+            gate(l7, h, NH)
+            if h > 0:
+                quant_h(l7, h - 1, NH)
+        quant_h(l7, NH - 1, NH)
+        for h in range(NH):
+            for i in range(h * 4 // NH, (h + 1) * 4 // NH):
+                s2_mm(l7, i)
+                ao(l7, i, i % 2 == 1)
+            store(l7, h, NH)

@@ -18,7 +18,7 @@ T = 512
 C = 512
 J = 4
 EPS = 1e-8
-PADC = 16
+PADW = 8
 FLOPS = 4 * 2 * B * T * C * C
 MANUAL = True
 QPOS = (10, 11, 12, 12)
@@ -76,6 +76,8 @@ def tile_rwkv_timemix_pa_t_kernel(
 
         ident = const.tile([P, P], BF16)
         masks.make_identity(nc, ident[:])
+        identf = const.tile([P, P], F32)
+        nc.vector.tensor_copy(out=identf[:], in_=ident[:])
         it_i = const.tile([P, T], I32)
         nc.gpsimd.iota(it_i[:], pattern=[[1, T]], base=1, channel_multiplier=0)
         half = const.tile([P, 1], F32)
@@ -132,23 +134,28 @@ def tile_rwkv_timemix_pa_t_kernel(
             )
 
         def transposes(b, halves):
-            for jh in halves:
-                xt = bank([P, 2, T], BF16, "xt")
-                xtp[(b, jh)] = xt
-                for jj in range(2):
-                    j = 2 * jh + jj
-                    for i in range(4):
-                        nc.tensor.transpose(
-                            out=xt[:, jj, i * P : (i + 1) * P],
-                            in_=xn[b][:, i, j:C:J],
-                            identity=ident[:],
-                        )
+            words = xn[b][:].rearrange("p i c -> p (i c)").bitcast(F32)
+            for u in halves:
+                xt = bank([P, T], F32, "xt")
+                xtp[(b, u)] = xt
+                for i in range(4):
+                    nc.tensor.transpose(
+                        out=xt[:, i * P : (i + 1) * P],
+                        in_=words[:, i * 256 + u : (i + 1) * 256 : 2],
+                        identity=identf[:],
+                    )
+
+        def pad_xT(b):
+            xT[b] = work.tile([P, 2, PADW + T, 2], BF16, name="xT", tag="xT", bufs=2)
+            nc.gpsimd.tensor_copy(
+                out=xT[b][:, :, PADW - 1, :], in_=xpT[:, :, b].rearrange("p (u e) -> p u e", e=2)
+            )
 
         def evac_xT(b):
-            xT[b] = work.tile([P, J, PADC + T], BF16, name="xT", tag="xT", bufs=2)
-            nc.gpsimd.tensor_copy(out=xT[b][:, :, PADC - 1 : PADC], in_=xpT[:, :, b : b + 1])
-            for jh in range(2):
-                nc.scalar.copy(out=xT[b][:, 2 * jh : 2 * jh + 2, PADC:], in_=xtp[(b, jh)][:])
+            words = xT[b][:].rearrange("p u t e -> p (u t e)").bitcast(F32)
+            for u in range(2):
+                w0 = u * (PADW + T) + PADW
+                nc.scalar.copy(out=words[:, w0 : w0 + T], in_=xtp[(b, u)][:])
 
         wc = {}
         ws = {}
@@ -156,18 +163,21 @@ def tile_rwkv_timemix_pa_t_kernel(
 
         def prep_w(key):
             wg[key] = const.tile([P, C, J], BF16, name="wg", tag="wg", bufs=3, align_bytes=64)
+            words = wnat[key][:].rearrange("p a c -> p (a c)").bitcast(F32)
+            grouped = wg[key][:].rearrange("p o j -> p (o j)").bitcast(F32)
             for h in range(2):
-                wt = bank([P, 2, J, P], BF16, "wt")
+                wt = bank([P, 2, 256], F32, "wt")
                 for a in range(2):
-                    for j in range(J):
+                    for u in range(2):
+                        w0 = (2 * h + a) * 256
                         nc.tensor.transpose(
-                            out=wt[:, a, j, :],
-                            in_=wnat[key][:, 2 * h + a, j:C:J],
-                            identity=ident[:],
+                            out=wt[:, u, a * P : (a + 1) * P],
+                            in_=words[:, w0 + u : w0 + 256 : 2],
+                            identity=identf[:],
                         )
                 nc.scalar.copy(
-                    out=wg[key][:, 256 * h : 256 * h + 256, :].rearrange("p (a o) j -> p a o j", a=2),
-                    in_=wt[:].rearrange("p a j o -> p a o j"),
+                    out=grouped[:, 512 * h : 512 * h + 512].rearrange("p (o u) -> p o u", u=2),
+                    in_=wt[:].rearrange("p u o -> p o u"),
                 )
 
         def quant_w(key):
@@ -193,9 +203,16 @@ def tile_rwkv_timemix_pa_t_kernel(
                 out=pl[m][:, j, :],
                 in0=dd[(b, j)][:],
                 scalar=pfa[:, j, mi : mi + 1],
-                in1=xT[b][:, j, PADC - 1 : PADC - 1 + T],
+                in1=xT[b][:, j // 2, PADW - 1 : PADW - 1 + T, j % 2],
                 op0=ALU.mult,
                 op1=ALU.add,
+            )
+
+        def regroup_scalar(m):
+            gr[m] = work.tile([P, T, J], BF16, name="gr", tag="gr", bufs=3, align_bytes=64)
+            nc.scalar.copy(
+                out=gr[m][:].rearrange("p (c i) t -> p c t i", i=4),
+                in_=pl[m][:].rearrange("p t (c i) -> p c t i", i=4),
             )
 
         def regroup(b, m, on_pool):
@@ -232,8 +249,8 @@ def tile_rwkv_timemix_pa_t_kernel(
 
         def alloc_b(b):
             ee[b] = work.tile([P, J, T], F32, name="ee", tag="ee", bufs=2)
-            th[b] = work.tile([P, J, T], F32, name="th", tag="th", bufs=2)
-            qq[b] = work.tile([P, J, T], F32, name="qq", tag="qq", bufs=2)
+            th[b] = work.tile([P, J, T], F32, name="th", tag="th", bufs=3)
+            qq[b] = work.tile([P, J, T], F32, name="qq", tag="qq", bufs=3)
             dn[b] = work.tile([P, J, T], F32, name="dn", tag="dn", bufs=2)
 
         def s1_mm(b, j, m):
@@ -299,8 +316,8 @@ def tile_rwkv_timemix_pa_t_kernel(
                 bias=g0h[:, j, b : b + 1],
             )
 
-        def y_dve(b, j):
-            nc.vector.tensor_scalar(
+        def y_on(b, j, eng):
+            eng.tensor_scalar(
                 out=qq[b][:, j, :],
                 in0=qq[b][:, j, :],
                 scalar1=half[:, 0:1],
@@ -354,7 +371,7 @@ def tile_rwkv_timemix_pa_t_kernel(
 
         def ao(b, i, on_vector):
             if i == 0:
-                ost[b] = work.tile([P, 4, C], F32, name="ost", tag="ost", bufs=2)
+                ost[b] = work.tile([P, 4, C], F32, name="ost", tag="ost", bufs=3)
             if on_vector:
                 nc.vector.tensor_copy(out=ost[b][:, i, :], in_=po[(b, i)][:])
             else:
@@ -380,36 +397,53 @@ def tile_rwkv_timemix_pa_t_kernel(
         transposes(0, (1,))
         make_dd(0, 2)
         make_dd(0, 3)
+        pad_xT(0)
         evac_xT(0)
-        ptb = bank([P, J, P], BF16, "ptb")
-        for j in range(J):
-            nc.tensor.transpose(out=ptb[:, j, :], in_=prmb[:, j:C:J], identity=ident[:])
-        pfb = const.tile([P, J, 24], F32)
-        nc.vector.tensor_copy(out=pfb[:], in_=ptb[:, :, 0:24])
-        negw = const.tile([P, J], F32)
-        nc.vector.tensor_scalar(out=negw[:], in0=pfb[:, :, 0], scalar1=-1.0, scalar2=None, op0=ALU.mult)
-        rb0 = const.tile([P, J, B], F32)
-        nc.vector.reciprocal(out=rb0[:], in_=pfb[:, :, 16:24])
-        g0 = const.tile([P, J, B], F32)
-        nc.vector.tensor_tensor(out=g0[:], in0=pfb[:, :, 8:16], in1=rb0[:], op=ALU.mult)
-        et = const.tile([P, J, B], F32)
-        nc.vector.tensor_scalar(out=et[:], in0=rb0[:], scalar1=EPS, scalar2=None, op0=ALU.mult)
-        g0e = const.tile([P, J, B], F32)
-        nc.vector.tensor_tensor(out=g0e[:], in0=g0[:], in1=et[:], op=ALU.mult)
-        g0h = const.tile([P, J, B], F32)
-        nc.vector.tensor_scalar(out=g0h[:], in0=g0[:], scalar1=0.5, scalar2=None, op0=ALU.mult)
-        lnb = const.tile([P, J, B], F32)
-        nc.scalar.activation(out=lnb[:], in_=pfb[:, :, 16:24], func=AF.Ln)
         dtab = const.tile([P, J, T], F32)
         beta = const.tile([P, J, B], F32)
 
+        pfb = const.tile([P, J, 24], F32)
+        negw = const.tile([P, J], F32)
+        rb0 = const.tile([P, J, B], F32)
+        g0 = const.tile([P, J, B], F32)
+        et = const.tile([P, J, B], F32)
+        g0e = const.tile([P, J, B], F32)
+        g0h = const.tile([P, J, B], F32)
+        lnb = const.tile([P, J, B], F32)
+
+        def params_pe():
+            ptb = bank([P, J, P], BF16, "ptb")
+            for j in range(J):
+                nc.tensor.transpose(out=ptb[:, j, :], in_=prmb[:, j:C:J], identity=ident[:])
+            return ptb
+
+        def params(ptb):
+            nc.vector.tensor_copy(out=pfb[:], in_=ptb[:, :, 0:24])
+            nc.vector.tensor_scalar(out=negw[:], in0=pfb[:, :, 0], scalar1=-1.0, scalar2=None, op0=ALU.mult)
+            nc.vector.reciprocal(out=rb0[:], in_=pfb[:, :, 16:24])
+            nc.vector.tensor_tensor(out=g0[:], in0=pfb[:, :, 8:16], in1=rb0[:], op=ALU.mult)
+            nc.vector.tensor_scalar(out=et[:], in0=rb0[:], scalar1=EPS, scalar2=None, op0=ALU.mult)
+            nc.vector.tensor_tensor(out=g0e[:], in0=g0[:], in1=et[:], op=ALU.mult)
+            nc.vector.tensor_scalar(out=g0h[:], in0=g0[:], scalar1=0.5, scalar2=None, op0=ALU.mult)
+            nc.scalar.activation(out=lnb[:], in_=pfb[:, :, 16:24], func=AF.Ln)
+
+        LNS = {2: (0, 1), 4: (2, 3), 6: (4, 5), 7: (6,)}
+        SCALAR_R = (3, 5)
+        SCALAR_V = (3, 5)
+        ORDER0 = [(mi, j) for jh in (0, 2) for mi in (1, 0, 2) for j in (jh, jh + 1)]
+        ORDER = [(mi, j) for mi in (1, 0, 2) for j in range(J)]
         for m in range(B):
             has_n = m + 1 < B
             h1 = m >= 1
-            h2 = m >= 2
             h3 = m >= 3
+            lns = LNS.get(m, ())
             if h1 and m + 2 < B:
                 load_x(m + 2, nc.sync)
+            if has_n:
+                pad_xT(m + 1)
+            if h3:
+                for j in range(J):
+                    y_on(m - 3, j, nc.gpsimd)
             if h1:
                 alloc_b(m - 1)
                 for j in range(J):
@@ -431,52 +465,58 @@ def tile_rwkv_timemix_pa_t_kernel(
                     d_q(m - 1, qd)
                     qd += 1
                 if s < 12:
-                    mix(m, s % 4, (1, 0, 2)[s // 4])
-                    if s >= 8 and has_n:
-                        make_dd(m + 1, s % 4)
-                    if s == 3:
+                    mi, j = (ORDER if h1 else ORDER0)[s]
+                    mix(m, j, mi)
+                    if h1 and s >= 8 and has_n:
+                        make_dd(m + 1, j)
+                    if s == (3 if h1 else 7):
                         regroup(m, "k", True)
-                    if s == 7 and m == 0:
+                    if s == 9 and m == 0:
                         regroup(m, "r", True)
                 if m == 0 and s == 2:
+                    ptb = params_pe()
                     prep_w("k")
                     transposes(1, (0, 1))
                     evac_xT(1)
                     prep_w("r")
                 if m == 0 and s == 8:
                     prep_w("v")
-            if h1:
+            if m == 0:
+                params(ptb)
                 for j in range(J):
-                    a_ln(m - 1, j)
-            if h3:
-                for i in range(4):
-                    s2_mm(m - 3, i)
-                    ao(m - 3, i, False)
-                store(m - 3, 0, 1)
+                    make_dd(1, j)
+            if m in SCALAR_R:
+                regroup_scalar("r")
+            for b in lns:
+                for j in range(J):
+                    a_ln(b, j)
             if m == 1:
                 prep_w("o")
-            if h2:
-                for j in range(J):
-                    d_x(m - 2, j)
-                for j in range(J):
-                    y_act(m - 2, j)
+            if m in SCALAR_V:
+                regroup_scalar("v")
             if h1 and has_n:
                 transposes(m + 1, (0, 1))
                 evac_xT(m + 1)
-            if h1:
-                a_rho(m - 1)
+            for b in lns:
+                a_rho(b)
+            if m >= 4:
+                for i in range(4):
+                    s2_mm(m - 4, i)
+                    ao(m - 4, i, False)
+                store(m - 4, 0, 1)
             if m == 0:
                 nc.vector.tensor_tensor(
                     out=beta[:], in0=pfb[:, :, 1:2].to_broadcast([P, J, B]), in1=lnb[:], op=ALU.subtract
                 )
-            if m > 0:
+            if m > 0 and m not in SCALAR_R:
                 regroup(m, "r", False)
-            regroup(m, "v", False)
+            if m not in SCALAR_V:
+                regroup(m, "v", False)
             if m == 0:
                 quant_w("k")
             quant_x(m, "k")
-            if h2:
-                gate(m - 2, 0, 1)
+            if h3:
+                gate(m - 3, 0, 1)
             if m == 0:
                 quant_w("r")
             quant_x(m, "r")
@@ -485,55 +525,64 @@ def tile_rwkv_timemix_pa_t_kernel(
             if m == 1:
                 quant_w("o")
             quant_x(m, "v")
-            if h2:
-                quant_h(m - 2, 0, 1)
+            if m >= 2:
+                for j in range(J):
+                    d_x(m - 2, j)
+            if h3:
+                quant_h(m - 3, 0, 1)
 
         l7 = B - 1
         l6 = B - 2
         l5 = B - 3
+        l4 = B - 4
+        for j in range(J):
+            y_on(l5, j, nc.gpsimd)
         alloc_b(l7)
         for j in range(J):
             s1_mm(l7, j, "k")
         for j in range(J):
             e_exp(l7, j)
             den(l7, j, nc.vector)
-        for j in range(J):
             s1_mm(l7, j, "v")
+        for j in range(J):
+            d_x(l6, j)
+        for j in range(J):
+            y_on(l6, j, nc.gpsimd)
         for j in range(J):
             d_q(l7, j)
         for j in range(J):
             a_ln(l7, j)
-        for j in range(J):
-            d_x(l6, j)
-        for j in range(J):
-            y_dve(l6, j)
+        for i in range(4):
+            s2_mm(l4, i)
+            ao(l4, i, False)
+        store(l4, 0, 1)
+        gate(l5, 0, 1)
+        quant_h(l5, 0, 1)
         for j in range(J):
             a_rhoj(l7, j)
         for j in range(J):
             s1_mm(l7, j, "r")
         for j in range(J):
             e_tanh(l7, j)
+        for j in range(J):
+            d_x(l7, j)
+        for j in range(J):
+            y_act(l7, j)
+        gate(l6, 0, 1)
+        quant_h(l6, 0, 1)
         for i in range(4):
             s2_mm(l5, i)
             ao(l5, i, False)
         store(l5, 0, 1)
-        gate(l6, 0, 1)
-        d_x(l7, 0)
-        d_x(l7, 1)
-        quant_h(l6, 0, 1)
-        d_x(l7, 2)
-        d_x(l7, 3)
-        for j in range(J):
-            y_dve(l7, j)
-        for i in range(4):
-            s2_mm(l6, i)
-            ao(l6, i, False)
-        store(l6, 0, 1)
         for h in range(NH):
             gate(l7, h, NH)
             if h > 0:
                 quant_h(l7, h - 1, NH)
         quant_h(l7, NH - 1, NH)
+        for i in range(4):
+            s2_mm(l6, i)
+            ao(l6, i, False)
+        store(l6, 0, 1)
         for h in range(NH):
             for i in range(h * 4 // NH, (h + 1) * 4 // NH):
                 s2_mm(l7, i)

@@ -208,12 +208,24 @@ def tile_rwkv_timemix_pa_t_kernel(
                 op1=ALU.add,
             )
 
-        def regroup_scalar(m):
-            gr[m] = work.tile([P, T, J], BF16, name="gr", tag="gr", bufs=3, align_bytes=64)
-            nc.scalar.copy(
-                out=gr[m][:].rearrange("p (c i) t -> p c t i", i=4),
-                in_=pl[m][:].rearrange("p t (c i) -> p c t i", i=4),
-            )
+        def regroup_part(m, t0, t1, eng):
+            if t0 == 0:
+                gr[m] = work.tile([P, T, J], BF16, name="gr", tag="gr", bufs=3, align_bytes=64)
+            if eng == "gpsimd":
+                nc.gpsimd.tensor_scalar(
+                    out=gr[m][:, t0:t1, :],
+                    in0=pl[m][:, :, t0:t1].rearrange("p t w -> p w t"),
+                    scalar1=1.0,
+                    scalar2=0.0,
+                    op0=ALU.mult,
+                    op1=ALU.add,
+                )
+            else:
+                copy = nc.scalar.copy if eng == "scalar" else nc.vector.tensor_copy
+                copy(
+                    out=gr[m][:, t0:t1, :].rearrange("p (c i) t -> p c t i", i=4),
+                    in_=pl[m][:, :, t0:t1].rearrange("p t (c i) -> p c t i", i=4),
+                )
 
         def regroup(b, m, on_pool):
             gr[m] = work.tile([P, T, J], BF16, name="gr", tag="gr", bufs=3, align_bytes=64)
@@ -428,8 +440,10 @@ def tile_rwkv_timemix_pa_t_kernel(
             nc.scalar.activation(out=lnb[:], in_=pfb[:, :, 16:24], func=AF.Ln)
 
         LNS = {2: (0, 1), 4: (2, 3), 6: (4, 5), 7: (6,)}
-        SCALAR_R = (3, 5)
+        RG = 256
+        SCALAR_R = (1, 3, 5)
         SCALAR_V = (3, 5)
+        Y_VECTOR = ()
         ORDER0 = [(mi, j) for jh in (0, 2) for mi in (1, 0, 2) for j in (jh, jh + 1)]
         ORDER = [(mi, j) for mi in (1, 0, 2) for j in range(J)]
         for m in range(B):
@@ -441,9 +455,9 @@ def tile_rwkv_timemix_pa_t_kernel(
                 load_x(m + 2, nc.sync)
             if has_n:
                 pad_xT(m + 1)
-            if h3:
+            if h3 and m in Y_VECTOR:
                 for j in range(J):
-                    y_on(m - 3, j, nc.gpsimd)
+                    y_on(m - 3, j, nc.vector)
             if h1:
                 alloc_b(m - 1)
                 for j in range(J):
@@ -459,6 +473,9 @@ def tile_rwkv_timemix_pa_t_kernel(
                 for j in range(J):
                     e_tanh(m - 1, j)
                     s1_mm(m - 1, j, "v")
+            if h3 and m not in Y_VECTOR:
+                for j in range(J):
+                    y_act(m - 3, j)
             qd = 0
             for s in range(13):
                 while h1 and qd < J and QPOS[qd] <= s:
@@ -470,9 +487,11 @@ def tile_rwkv_timemix_pa_t_kernel(
                     if h1 and s >= 8 and has_n:
                         make_dd(m + 1, j)
                     if s == (3 if h1 else 7):
-                        regroup(m, "k", True)
+                        regroup_part("k", 0, T, "gpsimd")
+                    if s == 7 and h1:
+                        regroup_part("r", 0, RG, "gpsimd")
                     if s == 9 and m == 0:
-                        regroup(m, "r", True)
+                        regroup_part("r", 0, T, "gpsimd")
                 if m == 0 and s == 2:
                     ptb = params_pe()
                     prep_w("k")
@@ -481,19 +500,20 @@ def tile_rwkv_timemix_pa_t_kernel(
                     prep_w("r")
                 if m == 0 and s == 8:
                     prep_w("v")
+                if m == 0 and s == 5:
+                    params(ptb)
             if m == 0:
-                params(ptb)
                 for j in range(J):
                     make_dd(1, j)
             if m in SCALAR_R:
-                regroup_scalar("r")
+                regroup_part("r", RG, T, "scalar")
             for b in lns:
                 for j in range(J):
                     a_ln(b, j)
             if m == 1:
                 prep_w("o")
             if m in SCALAR_V:
-                regroup_scalar("v")
+                regroup_part("v", 0, T, "scalar")
             if h1 and has_n:
                 transposes(m + 1, (0, 1))
                 evac_xT(m + 1)
@@ -509,9 +529,9 @@ def tile_rwkv_timemix_pa_t_kernel(
                     out=beta[:], in0=pfb[:, :, 1:2].to_broadcast([P, J, B]), in1=lnb[:], op=ALU.subtract
                 )
             if m > 0 and m not in SCALAR_R:
-                regroup(m, "r", False)
+                regroup_part("r", RG, T, "vector")
             if m not in SCALAR_V:
-                regroup(m, "v", False)
+                regroup_part("v", 0, T, "vector")
             if m == 0:
                 quant_w("k")
             quant_x(m, "k")
@@ -535,8 +555,6 @@ def tile_rwkv_timemix_pa_t_kernel(
         l6 = B - 2
         l5 = B - 3
         l4 = B - 4
-        for j in range(J):
-            y_on(l5, j, nc.gpsimd)
         alloc_b(l7)
         for j in range(J):
             s1_mm(l7, j, "k")
@@ -547,23 +565,25 @@ def tile_rwkv_timemix_pa_t_kernel(
         for j in range(J):
             d_x(l6, j)
         for j in range(J):
-            y_on(l6, j, nc.gpsimd)
+            y_act(l5, j)
         for j in range(J):
             d_q(l7, j)
         for j in range(J):
             a_ln(l7, j)
-        for i in range(4):
-            s2_mm(l4, i)
-            ao(l4, i, False)
-        store(l4, 0, 1)
         gate(l5, 0, 1)
         quant_h(l5, 0, 1)
+        for j in range(J):
+            y_on(l6, j, nc.vector)
         for j in range(J):
             a_rhoj(l7, j)
         for j in range(J):
             s1_mm(l7, j, "r")
         for j in range(J):
             e_tanh(l7, j)
+        for i in range(4):
+            s2_mm(l4, i)
+            ao(l4, i, False)
+        store(l4, 0, 1)
         for j in range(J):
             d_x(l7, j)
         for j in range(J):

@@ -70,8 +70,8 @@ def tile_rwkv_timemix_pa_t_kernel(
         xn[0] = work.tile([P, 4, C], BF16, name="xn", tag="xn", bufs=3)
         for hh in range(2):
             nc.sync.dma_start(
-                out=xn[0][:, :, hh * 256 : (hh + 1) * 256],
-                in_=x[0, :, hh * 256 : (hh + 1) * 256].rearrange("(i p) c -> p i c", p=P),
+                out=xn[0][:, 2 * hh : 2 * hh + 2, :],
+                in_=x[0, hh * 256 : (hh + 1) * 256, :].rearrange("(i p) c -> p i c", p=P),
             )
 
         ident = const.tile([P, P], BF16)
@@ -107,6 +107,7 @@ def tile_rwkv_timemix_pa_t_kernel(
             scalar2=None,
             op0=ALU.mult,
         )
+
         it_f = const.tile([P, T], F32)
         nc.vector.tensor_copy(out=it_f[:], in_=it_i[:])
 
@@ -263,7 +264,7 @@ def tile_rwkv_timemix_pa_t_kernel(
             ee[b] = work.tile([P, J, T], F32, name="ee", tag="ee", bufs=2)
             th[b] = work.tile([P, J, T], F32, name="th", tag="th", bufs=3)
             qq[b] = work.tile([P, J, T], F32, name="qq", tag="qq", bufs=3)
-            dn[b] = work.tile([P, J, T], F32, name="dn", tag="dn", bufs=2)
+            dn[b] = work.tile([P, J, T], F32, name="dn", tag="dn", bufs=3)
 
         def s1_mm(b, j, m):
             ps[(b, j, m)] = bank([P, T], F32, "s1" + m)
@@ -383,7 +384,7 @@ def tile_rwkv_timemix_pa_t_kernel(
 
         def ao(b, i, on_vector):
             if i == 0:
-                ost[b] = work.tile([P, 4, C], F32, name="ost", tag="ost", bufs=3)
+                ost[b] = work.tile([P, 4, C], F32, name="ost", tag="ost", bufs=2)
             if on_vector:
                 nc.vector.tensor_copy(out=ost[b][:, i, :], in_=po[(b, i)][:])
             else:
@@ -442,7 +443,7 @@ def tile_rwkv_timemix_pa_t_kernel(
         LNS = {2: (0, 1), 4: (2, 3), 6: (4, 5), 7: (6,)}
         RG = 256
         SCALAR_R = (1, 3, 5)
-        SCALAR_V = (3, 5)
+        SCALAR_V = (0, 3)
         Y_VECTOR = ()
         ORDER0 = [(mi, j) for jh in (0, 2) for mi in (1, 0, 2) for j in (jh, jh + 1)]
         ORDER = [(mi, j) for mi in (1, 0, 2) for j in range(J)]
@@ -565,7 +566,7 @@ def tile_rwkv_timemix_pa_t_kernel(
         for j in range(J):
             d_x(l6, j)
         for j in range(J):
-            y_act(l5, j)
+            y_on(l5, j, nc.vector)
         for j in range(J):
             d_q(l7, j)
         for j in range(J):

@@ -152,11 +152,12 @@ def tile_rwkv_timemix_pa_t_kernel(
                 out=xT[b][:, :, PADW - 1, :], in_=xpT[:, :, b].rearrange("p (u e) -> p u e", e=2)
             )
 
-        def evac_xT(b):
+        def evac_xT(b, on_vector=False):
+            copy = nc.vector.tensor_copy if on_vector else nc.scalar.copy
             words = xT[b][:].rearrange("p u t e -> p (u t e)").bitcast(F32)
             for u in range(2):
                 w0 = u * (PADW + T) + PADW
-                nc.scalar.copy(out=words[:, w0 : w0 + T], in_=xtp[(b, u)][:])
+                copy(out=words[:, w0 : w0 + T], in_=xtp[(b, u)][:])
 
         wc = {}
         ws = {}
@@ -264,7 +265,7 @@ def tile_rwkv_timemix_pa_t_kernel(
             ee[b] = work.tile([P, J, T], F32, name="ee", tag="ee", bufs=2)
             th[b] = work.tile([P, J, T], F32, name="th", tag="th", bufs=3)
             qq[b] = work.tile([P, J, T], F32, name="qq", tag="qq", bufs=3)
-            dn[b] = work.tile([P, J, T], F32, name="dn", tag="dn", bufs=3)
+            dn[b] = work.tile([P, J, T], F32, name="dn", tag="dn", bufs=2)
 
         def s1_mm(b, j, m):
             ps[(b, j, m)] = bank([P, T], F32, "s1" + m)
@@ -384,7 +385,7 @@ def tile_rwkv_timemix_pa_t_kernel(
 
         def ao(b, i, on_vector):
             if i == 0:
-                ost[b] = work.tile([P, 4, C], F32, name="ost", tag="ost", bufs=2)
+                ost[b] = work.tile([P, 4, C], F32, name="ost", tag="ost", bufs=3)
             if on_vector:
                 nc.vector.tensor_copy(out=ost[b][:, i, :], in_=po[(b, i)][:])
             else:
@@ -441,8 +442,10 @@ def tile_rwkv_timemix_pa_t_kernel(
             nc.scalar.activation(out=lnb[:], in_=pfb[:, :, 16:24], func=AF.Ln)
 
         LNS = {2: (0, 1), 4: (2, 3), 6: (4, 5), 7: (6,)}
-        RG = 256
-        SCALAR_R = (1, 3, 5)
+        RG = (0, 0, 256, 0, 256, 0, 256, 0)
+        EVAC_V = (2, 4, 6)
+        AO_V = ()
+        SCALAR_R = (3, 5)
         SCALAR_V = (0, 3)
         Y_VECTOR = ()
         ORDER0 = [(mi, j) for jh in (0, 2) for mi in (1, 0, 2) for j in (jh, jh + 1)]
@@ -489,8 +492,8 @@ def tile_rwkv_timemix_pa_t_kernel(
                         make_dd(m + 1, j)
                     if s == (3 if h1 else 7):
                         regroup_part("k", 0, T, "gpsimd")
-                    if s == 7 and h1:
-                        regroup_part("r", 0, RG, "gpsimd")
+                    if s == 7 and h1 and RG[m] > 0:
+                        regroup_part("r", 0, RG[m], "gpsimd")
                     if s == 9 and m == 0:
                         regroup_part("r", 0, T, "gpsimd")
                 if m == 0 and s == 2:
@@ -507,7 +510,7 @@ def tile_rwkv_timemix_pa_t_kernel(
                 for j in range(J):
                     make_dd(1, j)
             if m in SCALAR_R:
-                regroup_part("r", RG, T, "scalar")
+                regroup_part("r", RG[m], T, "scalar")
             for b in lns:
                 for j in range(J):
                     a_ln(b, j)
@@ -517,20 +520,20 @@ def tile_rwkv_timemix_pa_t_kernel(
                 regroup_part("v", 0, T, "scalar")
             if h1 and has_n:
                 transposes(m + 1, (0, 1))
-                evac_xT(m + 1)
+                evac_xT(m + 1, m in EVAC_V)
             for b in lns:
                 a_rho(b)
             if m >= 4:
                 for i in range(4):
                     s2_mm(m - 4, i)
-                    ao(m - 4, i, False)
+                    ao(m - 4, i, m in AO_V and i % 2 == 1)
                 store(m - 4, 0, 1)
             if m == 0:
                 nc.vector.tensor_tensor(
                     out=beta[:], in0=pfb[:, :, 1:2].to_broadcast([P, J, B]), in1=lnb[:], op=ALU.subtract
                 )
             if m > 0 and m not in SCALAR_R:
-                regroup_part("r", RG, T, "vector")
+                regroup_part("r", RG[m], T, "vector")
             if m not in SCALAR_V:
                 regroup_part("v", 0, T, "vector")
             if m == 0:

@@ -222,9 +222,12 @@ def tile_rwkv_timemix_pa_t_kernel(
                     op0=ALU.mult,
                     op1=ALU.add,
                 )
+            elif eng == "scalar":
+                nc.scalar.copy(
+                    out=gr[m][:, t0:t1, :], in_=pl[m][:, :, t0:t1].rearrange("p t w -> p w t")
+                )
             else:
-                copy = nc.scalar.copy if eng == "scalar" else nc.vector.tensor_copy
-                copy(
+                nc.vector.tensor_copy(
                     out=gr[m][:, t0:t1, :].rearrange("p (c i) t -> p c t i", i=4),
                     in_=pl[m][:, :, t0:t1].rearrange("p t (c i) -> p c t i", i=4),
                 )
@@ -441,12 +444,13 @@ def tile_rwkv_timemix_pa_t_kernel(
             nc.vector.tensor_scalar(out=g0h[:], in0=g0[:], scalar1=0.5, scalar2=None, op0=ALU.mult)
             nc.scalar.activation(out=lnb[:], in_=pfb[:, :, 16:24], func=AF.Ln)
 
-        LNS = {2: (0, 1), 4: (2, 3), 6: (4, 5), 7: (6,)}
-        RG = (0, 0, 256, 0, 256, 0, 256, 0)
-        EVAC_V = (2, 4, 6)
+        LNS = {1: (0,), 3: (1, 2), 5: (3, 4), 7: (5, 6)}
+        RG = (0, 0, 0, 256, 0, 256, 0, 256)
+        EVAC_V = ()
         AO_V = ()
-        SCALAR_R = (3, 5)
-        SCALAR_V = (0, 3)
+        LIGHT = (2, 4, 6)
+        SCALAR_R = (2, 4, 6)
+        SCALAR_V = ()
         Y_VECTOR = ()
         ORDER0 = [(mi, j) for jh in (0, 2) for mi in (1, 0, 2) for j in (jh, jh + 1)]
         ORDER = [(mi, j) for mi in (1, 0, 2) for j in range(J)]
@@ -472,7 +476,8 @@ def tile_rwkv_timemix_pa_t_kernel(
                         nc.scalar.activation(
                             out=dtab[:, j, :], in_=it_f[:], func=AF.Exp, scale=negw[:, j : j + 1]
                         )
-                    den(m - 1, j, nc.gpsimd)
+                    if m not in LIGHT:
+                        den(m - 1, j, nc.gpsimd)
                     s1_mm(m - 1, j, "r")
                 for j in range(J):
                     e_tanh(m - 1, j)
@@ -492,10 +497,11 @@ def tile_rwkv_timemix_pa_t_kernel(
                         make_dd(m + 1, j)
                     if s == (3 if h1 else 7):
                         regroup_part("k", 0, T, "gpsimd")
+                        if m in LIGHT:
+                            for j2 in range(J):
+                                den(m - 1, j2, nc.gpsimd)
                     if s == 7 and h1 and RG[m] > 0:
                         regroup_part("r", 0, RG[m], "gpsimd")
-                    if s == 9 and m == 0:
-                        regroup_part("r", 0, T, "gpsimd")
                 if m == 0 and s == 2:
                     ptb = params_pe()
                     prep_w("k")
@@ -523,7 +529,7 @@ def tile_rwkv_timemix_pa_t_kernel(
                 evac_xT(m + 1, m in EVAC_V)
             for b in lns:
                 a_rho(b)
-            if m >= 4:
+            if 4 <= m < B - 1:
                 for i in range(4):
                     s2_mm(m - 4, i)
                     ao(m - 4, i, m in AO_V and i % 2 == 1)
@@ -532,7 +538,7 @@ def tile_rwkv_timemix_pa_t_kernel(
                 nc.vector.tensor_tensor(
                     out=beta[:], in0=pfb[:, :, 1:2].to_broadcast([P, J, B]), in1=lnb[:], op=ALU.subtract
                 )
-            if m > 0 and m not in SCALAR_R:
+            if m not in SCALAR_R:
                 regroup_part("r", RG[m], T, "vector")
             if m not in SCALAR_V:
                 regroup_part("v", 0, T, "vector")
@@ -566,6 +572,10 @@ def tile_rwkv_timemix_pa_t_kernel(
             e_exp(l7, j)
             den(l7, j, nc.vector)
             s1_mm(l7, j, "v")
+        for i in range(4):
+            s2_mm(B - 5, i)
+            ao(B - 5, i, False)
+        store(B - 5, 0, 1)
         for j in range(J):
             d_x(l6, j)
         for j in range(J):

@@ -222,12 +222,9 @@ def tile_rwkv_timemix_pa_t_kernel(
                     op0=ALU.mult,
                     op1=ALU.add,
                 )
-            elif eng == "scalar":
-                nc.scalar.copy(
-                    out=gr[m][:, t0:t1, :], in_=pl[m][:, :, t0:t1].rearrange("p t w -> p w t")
-                )
             else:
-                nc.vector.tensor_copy(
+                copy = nc.scalar.copy if eng == "scalar" else nc.vector.tensor_copy
+                copy(
                     out=gr[m][:, t0:t1, :].rearrange("p (c i) t -> p c t i", i=4),
                     in_=pl[m][:, :, t0:t1].rearrange("p t (c i) -> p c t i", i=4),
                 )
@@ -445,12 +442,12 @@ def tile_rwkv_timemix_pa_t_kernel(
             nc.scalar.activation(out=lnb[:], in_=pfb[:, :, 16:24], func=AF.Ln)
 
         LNS = {1: (0,), 3: (1, 2), 5: (3, 4), 7: (5, 6)}
-        RG = (0, 0, 0, 256, 0, 256, 0, 256)
+        RG = (0,) * 8
         EVAC_V = ()
         AO_V = ()
         LIGHT = (2, 4, 6)
         SCALAR_R = (2, 4, 6)
-        SCALAR_V = ()
+        SCALAR_V = (0, 4)
         Y_VECTOR = ()
         ORDER0 = [(mi, j) for jh in (0, 2) for mi in (1, 0, 2) for j in (jh, jh + 1)]
         ORDER = [(mi, j) for mi in (1, 0, 2) for j in range(J)]
@@ -597,7 +594,8 @@ def tile_rwkv_timemix_pa_t_kernel(
         for i in range(4):
             s2_mm(l4, i)
             ao(l4, i, False)
-        store(l4, 0, 1)
+            if i % 2 == 1:
+                store(l4, i // 2, 2)
         for j in range(J):
             d_x(l7, j)
         for j in range(J):
@@ -607,7 +605,8 @@ def tile_rwkv_timemix_pa_t_kernel(
         for i in range(4):
             s2_mm(l5, i)
             ao(l5, i, False)
-        store(l5, 0, 1)
+            if i % 2 == 1:
+                store(l5, i // 2, 2)
         for h in range(NH):
             gate(l7, h, NH)
             if h > 0:
@@ -616,7 +615,8 @@ def tile_rwkv_timemix_pa_t_kernel(
         for i in range(4):
             s2_mm(l6, i)
             ao(l6, i, False)
-        store(l6, 0, 1)
+            if i % 2 == 1:
+                store(l6, i // 2, 2)
         for h in range(NH):
             for i in range(h * 4 // NH, (h + 1) * 4 // NH):
                 s2_mm(l7, i)

@@ -39,6 +39,9 @@ def tile_rwkv_timemix_pa_t_kernel(
         def bank(shape, dtype, name):
             return psum.tile(shape, dtype, name=name, tag="ps", bufs=8)
 
+        half = const.tile([P, 1], F32)
+        nc.vector.memset(half[:], 0.5)
+        dummy = const.tile([P, 1], F32)
         prma = const.tile([P, C], BF16)
         prmb = const.tile([P, C], BF16)
         nc.vector.memset(prma[:], 0.0)
@@ -49,6 +52,7 @@ def tile_rwkv_timemix_pa_t_kernel(
         for r, vec in enumerate((mu_r, mu_k, mu_v)):
             nc.scalar.dma_start(out=prma[r : r + 1, :], in_=vec.rearrange("(o c) -> o c", o=1))
         nc.scalar.dma_start(out=prma[24:32, :], in_=x_prev0)
+        nc.scalar.activation(out=dummy[:], in_=half[:], func=AF.Ln)
         for r, vec in enumerate((w, u)):
             nc.scalar.dma_start(out=prmb[r : r + 1, :], in_=vec.rearrange("(o c) -> o c", o=1))
         nc.scalar.dma_start(out=prmb[8:16, :], in_=a0)
@@ -80,10 +84,6 @@ def tile_rwkv_timemix_pa_t_kernel(
         nc.vector.tensor_copy(out=identf[:], in_=ident[:])
         it_i = const.tile([P, T], I32)
         nc.gpsimd.iota(it_i[:], pattern=[[1, T]], base=1, channel_multiplier=0)
-        half = const.tile([P, 1], F32)
-        nc.vector.memset(half[:], 0.5)
-        dummy = const.tile([P, 1], F32)
-        nc.scalar.activation(out=dummy[:], in_=half[:], func=AF.Ln)
         load_w("k", W_k)
         load_w("r", W_r)
         load_w("v", W_v)
@@ -290,6 +290,9 @@ def tile_rwkv_timemix_pa_t_kernel(
         def den(b, j, eng):
             eng.tensor_tensor(out=dn[b][:, j, :], in0=ee[b][:, j, :], in1=dtab[:, j, :], op=ALU.add)
 
+        def den_all(b):
+            nc.gpsimd.tensor_tensor(out=dn[b][:], in0=ee[b][:], in1=dtab[:], op=ALU.add)
+
         def d_q(b, j):
             nc.vector.scalar_tensor_tensor(
                 out=qq[b][:, j, :],
@@ -447,7 +450,7 @@ def tile_rwkv_timemix_pa_t_kernel(
         AO_V = ()
         LIGHT = (2, 4, 6)
         SCALAR_R = (2, 4, 6)
-        SCALAR_V = (0, 4)
+        SCALAR_V = (4,)
         Y_VECTOR = ()
         ORDER0 = [(mi, j) for jh in (0, 2) for mi in (1, 0, 2) for j in (jh, jh + 1)]
         ORDER = [(mi, j) for mi in (1, 0, 2) for j in range(J)]
@@ -484,7 +487,7 @@ def tile_rwkv_timemix_pa_t_kernel(
                     y_act(m - 3, j)
             qd = 0
             for s in range(13):
-                while h1 and qd < J and QPOS[qd] <= s:
+                while h1 and qd < J and (12, 12, 12, 12)[qd] <= s:
                     d_q(m - 1, qd)
                     qd += 1
                 if s < 12:
@@ -502,13 +505,13 @@ def tile_rwkv_timemix_pa_t_kernel(
                 if m == 0 and s == 2:
                     ptb = params_pe()
                     prep_w("k")
+                if m == 0 and s == 5:
+                    params(ptb)
                     transposes(1, (0, 1))
                     evac_xT(1)
                     prep_w("r")
                 if m == 0 and s == 8:
                     prep_w("v")
-                if m == 0 and s == 5:
-                    params(ptb)
             if m == 0:
                 for j in range(J):
                     make_dd(1, j)

from contextlib import ExitStack

import concourse.masks as masks
import concourse.mybir as mybir

FP8X4 = mybir.dt.float8_e4m3fn_x4
BF16 = mybir.dt.bfloat16
F32 = mybir.dt.float32
I32 = mybir.dt.int32
U32 = mybir.dt.uint32
U8 = mybir.dt.uint8
ALU = mybir.AluOpType
AF = mybir.ActivationFunctionType

P = 128
B = 8
T = 512
C = 512
J = 4
EPS = 1e-8
PADW = 8
FLOPS = 4 * 2 * B * T * C * C
MANUAL = True
QPOS = (10, 11, 12, 12)
NH = 4


def tile_rwkv_timemix_pa_t_kernel(
    tc, x, a0, b0, x_prev0, w, u, mu_r, mu_k, mu_v, W_r, W_k, W_v, W_out, out
):
    nc = tc.nc
    with ExitStack() as ctx:
        if MANUAL:
            ctx.enter_context(tc.manual_schedule())
        const = ctx.enter_context(tc.tile_pool(name="const", bufs=1))
        work = ctx.enter_context(tc.tile_pool(name="work", bufs=2))
        psum = ctx.enter_context(tc.psum_pool(name="psum", bufs=8))

        def bank(shape, dtype, name):
            return psum.tile(shape, dtype, name=name, tag="ps", bufs=8)

        half = const.tile([P, 1], F32)
        nc.vector.memset(half[:], 0.5)
        dummy = const.tile([P, 1], F32)
        prma = const.tile([P, C], BF16)
        prmb = const.tile([P, C], BF16)
        nc.vector.memset(prma[:], 0.0)
        nc.vector.memset(prmb[:], 0.0)
        nc.sync.dma_start(
            out=prma[32:64, :], in_=x.rearrange("b (i t) c -> (b i) t c", t=P)[:, P - 1, :]
        )
        for r, vec in enumerate((mu_r, mu_k, mu_v)):
            nc.scalar.dma_start(out=prma[r : r + 1, :], in_=vec.rearrange("(o c) -> o c", o=1))
        nc.scalar.dma_start(out=prma[24:32, :], in_=x_prev0)
        nc.scalar.activation(out=dummy[:], in_=half[:], func=AF.Ln)
        for r, vec in enumerate((w, u)):
            nc.scalar.dma_start(out=prmb[r : r + 1, :], in_=vec.rearrange("(o c) -> o c", o=1))
        nc.scalar.dma_start(out=prmb[8:16, :], in_=a0)
        nc.scalar.dma_start(out=prmb[16:24, :], in_=b0)

        xn = {}

        def load_x(b, queue):
            xn[b] = work.tile([P, 4, C], BF16, name="xn", tag="xn", bufs=3)
            queue.dma_start(out=xn[b][:], in_=x[b].rearrange("(i p) c -> p i c", p=P))

        wnat = {}

        def load_w(key, wap):
            wnat[key] = const.tile([P, 4, C], BF16, name="wn" + key, tag="wn" + key)
            rows = "(a p) c -> p a c" if key == "o" else "(p a) c -> p a c"
            nc.scalar.dma_start(out=wnat[key][:], in_=wap.rearrange(rows, p=P))

        xn[0] = work.tile([P, 4, C], BF16, name="xn", tag="xn", bufs=3)
        for hh in range(2):
            nc.sync.dma_start(
                out=xn[0][:, 2 * hh : 2 * hh + 2, :],
                in_=x[0, hh * 256 : (hh + 1) * 256, :].rearrange("(i p) c -> p i c", p=P),
            )

        ident = const.tile([P, P], BF16)
        masks.make_identity(nc, ident[:])
        identf = const.tile([P, P], F32)
        nc.vector.tensor_copy(out=identf[:], in_=ident[:])
        it_i = const.tile([P, T], I32)
        nc.gpsimd.iota(it_i[:], pattern=[[1, T]], base=1, channel_multiplier=0)
        load_w("k", W_k)
        load_w("r", W_r)
        load_w("v", W_v)
        load_x(1, nc.scalar)
        load_w("o", W_out)
        load_x(2, nc.scalar)
        dmat = const.tile([P, P], BF16)
        nc.vector.tensor_copy(out=dmat[:, 0:1], in_=ident[:, 0:1])
        nc.vector.tensor_tensor(
            out=dmat[:, 1:P], in0=ident[:, 1:P], in1=ident[:, 0 : P - 1], op=ALU.subtract
        )
        sel = const.tile([P, B, 4, 8], BF16)
        nc.vector.memset(sel[:], 0.0)
        nc.vector.tensor_scalar(
            out=sel[:, :, 0, 0], in0=ident[:, 24:32], scalar1=-1.0, scalar2=None, op0=ALU.mult
        )
        nc.vector.tensor_scalar(
            out=sel[:, :, 1:4, 0],
            in0=ident[:, 32:64].rearrange("p (b i) -> p b i", i=4)[:, :, 0:3],
            scalar1=-1.0,
            scalar2=None,
            op0=ALU.mult,
        )

        it_f = const.tile([P, T], F32)
        nc.vector.tensor_copy(out=it_f[:], in_=it_i[:])

        xT = {}
        dd = {}
        xtp = {}

        def make_dd(b, j):
            t = bank([P, T], F32, "dd")
            dd[(b, j)] = t
            for i in range(4):
                nc.tensor.matmul(
                    out=t[:, i * P : (i + 1) * P],
                    lhsT=xn[b][:, i, j:C:J],
                    rhs=dmat[:],
                    start=(i == 0),
                    stop=False,
                )
            nc.tensor.matmul(
                out=t[:].rearrange("p (i e) -> p i e", e=P)[:, :, 0:8],
                lhsT=prma[:, j:C:J],
                rhs=sel[:, b, :, :],
                start=False,
                stop=True,
            )

        def transposes(b, halves):
            words = xn[b][:].rearrange("p i c -> p (i c)").bitcast(F32)
            for u in halves:
                xt = bank([P, T], F32, "xt")
                xtp[(b, u)] = xt
                for i in range(4):
                    nc.tensor.transpose(
                        out=xt[:, i * P : (i + 1) * P],
                        in_=words[:, i * 256 + u : (i + 1) * 256 : 2],
                        identity=identf[:],
                    )

        def pad_xT(b):
            xT[b] = work.tile([P, 2, PADW + T, 2], BF16, name="xT", tag="xT", bufs=2)
            nc.gpsimd.tensor_copy(
                out=xT[b][:, :, PADW - 1, :], in_=xpT[:, :, b].rearrange("p (u e) -> p u e", e=2)
            )

        def evac_xT(b, on_vector=False):
            copy = nc.vector.tensor_copy if on_vector else nc.scalar.copy
            words = xT[b][:].rearrange("p u t e -> p (u t e)").bitcast(F32)
            for u in range(2):
                w0 = u * (PADW + T) + PADW
                copy(out=words[:, w0 : w0 + T], in_=xtp[(b, u)][:])

        wc = {}
        ws = {}
        wg = {}

        def prep_w(key):
            wg[key] = const.tile([P, C, J], BF16, name="wg", tag="wg", bufs=3, align_bytes=64)
            words = wnat[key][:].rearrange("p a c -> p (a c)").bitcast(F32)
            grouped = wg[key][:].rearrange("p o j -> p (o j)").bitcast(F32)
            for h in range(2):
                wt = bank([P, 2, 256], F32, "wt")
                for a in range(2):
                    for u in range(2):
                        w0 = (2 * h + a) * 256
                        nc.tensor.transpose(
                            out=wt[:, u, a * P : (a + 1) * P],
                            in_=words[:, w0 + u : w0 + 256 : 2],
                            identity=identf[:],
                        )
                nc.scalar.copy(
                    out=grouped[:, 512 * h : 512 * h + 512].rearrange("p (o u) -> p o u", u=2),
                    in_=wt[:].rearrange("p u o -> p o u"),
                )

        def quant_w(key):
            wc[key] = const.tile([P, C], U32, name="wc" + key, tag="wc" + key, align_bytes=64)
            ws[key] = const.tile([P, C], U8, name="ws" + key, tag="ws" + key, align_bytes=64)
            nc.vector.quantize_mx(
                out=wc[key][:].bitcast(FP8X4),
                scales=ws[key][:],
                in_=wg[key][:].rearrange("p o j -> p (o j)"),
            )

        pl = {}
        gr = {}
        xc = {}
        xs = {}
        MS = ("r", "k", "v")

        def mix(b, j, mi):
            m = MS[mi]
            if j == 0:
                pl[m] = work.tile([P, J, T], BF16, name="pl" + m, tag="pl" + m, bufs=1)
            nc.vector.scalar_tensor_tensor(
                out=pl[m][:, j, :],
                in0=dd[(b, j)][:],
                scalar=pfa[:, j, mi : mi + 1],
                in1=xT[b][:, j // 2, PADW - 1 : PADW - 1 + T, j % 2],
                op0=ALU.mult,
                op1=ALU.add,
            )

        def regroup_part(m, t0, t1, eng):
            if t0 == 0:
                gr[m] = work.tile([P, T, J], BF16, name="gr", tag="gr", bufs=3, align_bytes=64)
            if eng == "gpsimd":
                nc.gpsimd.tensor_scalar(
                    out=gr[m][:, t0:t1, :],
                    in0=pl[m][:, :, t0:t1].rearrange("p t w -> p w t"),
                    scalar1=1.0,
                    scalar2=0.0,
                    op0=ALU.mult,
                    op1=ALU.add,
                )
            else:
                copy = nc.scalar.copy if eng == "scalar" else nc.vector.tensor_copy
                copy(
                    out=gr[m][:, t0:t1, :].rearrange("p (c i) t -> p c t i", i=4),
                    in_=pl[m][:, :, t0:t1].rearrange("p t (c i) -> p c t i", i=4),
                )

        def regroup(b, m, on_pool):
            gr[m] = work.tile([P, T, J], BF16, name="gr", tag="gr", bufs=3, align_bytes=64)
            if on_pool:
                nc.gpsimd.tensor_scalar(
                    out=gr[m][:],
                    in0=pl[m][:].rearrange("p t w -> p w t"),
                    scalar1=1.0,
                    scalar2=0.0,
                    op0=ALU.mult,
                    op1=ALU.add,
                )
            else:
                nc.vector.tensor_copy(
                    out=gr[m][:].rearrange("p (c i) t -> p c t i", i=4),
                    in_=pl[m][:].rearrange("p t (c i) -> p c t i", i=4),
                )

        def quant_x(b, m):
            xc[(b, m)] = work.tile([P, T], U32, name="xc" + m, tag="xc" + m, bufs=2, align_bytes=64)
            xs[(b, m)] = work.tile([P, T], U8, name="xs" + m, tag="xs" + m, bufs=2, align_bytes=64)
            nc.vector.quantize_mx(
                out=xc[(b, m)][:].bitcast(FP8X4),
                scales=xs[(b, m)][:],
                in_=gr[m][:].rearrange("p w t -> p (w t)"),
            )

        ee = {}
        th = {}
        qq = {}
        dn = {}
        ps = {}

        def alloc_b(b):
            ee[b] = work.tile([P, J, T], F32, name="ee", tag="ee", bufs=2)
            th[b] = work.tile([P, J, T], F32, name="th", tag="th", bufs=3)
            qq[b] = work.tile([P, J, T], F32, name="qq", tag="qq", bufs=3)
            dn[b] = work.tile([P, J, T], F32, name="dn", tag="dn", bufs=2)

        def s1_mm(b, j, m):
            ps[(b, j, m)] = bank([P, T], F32, "s1" + m)
            nc.tensor.matmul_mx(
                out=ps[(b, j, m)][:],
                lhsT=wc[m][:, j * P : (j + 1) * P].bitcast(FP8X4),
                lhsT_scale=ws[m][:, j * P : (j + 1) * P],
                rhs=xc[(b, m)][:].bitcast(FP8X4),
                rhs_scale=xs[(b, m)][:],
                start=True,
                stop=True,
            )

        def e_exp(b, j):
            nc.scalar.activation(
                out=ee[b][:, j, :], in_=ps[(b, j, "k")][:], func=AF.Exp, bias=beta[:, j, b : b + 1]
            )

        def e_tanh(b, j):
            nc.scalar.activation(out=th[b][:, j, :], in_=ps[(b, j, "r")][:], func=AF.Tanh, scale=0.5)

        def den(b, j, eng):
            eng.tensor_tensor(out=dn[b][:, j, :], in0=ee[b][:, j, :], in1=dtab[:, j, :], op=ALU.add)

        def den_all(b):
            nc.gpsimd.tensor_tensor(out=dn[b][:], in0=ee[b][:], in1=dtab[:], op=ALU.add)

        def d_q(b, j):
            nc.vector.scalar_tensor_tensor(
                out=qq[b][:, j, :],
                in0=ps[(b, j, "v")][:],
                scalar=g0[:, j, b : b + 1],
                in1=ee[b][:, j, :],
                op0=ALU.subtract,
                op1=ALU.mult,
            )

        def a_ln(b, j):
            nc.scalar.activation(
                out=dn[b][:, j, :], in_=dn[b][:, j, :], func=AF.Ln, bias=et[:, j, b : b + 1]
            )

        def a_rho(b):
            nc.scalar.activation(out=dn[b][:], in_=dn[b][:], func=AF.Exp, scale=-1.0)

        def a_rhoj(b, j):
            nc.scalar.activation(out=dn[b][:, j, :], in_=dn[b][:, j, :], func=AF.Exp, scale=-1.0)

        def d_x(b, j):
            nc.vector.scalar_tensor_tensor(
                out=qq[b][:, j, :],
                in0=qq[b][:, j, :],
                scalar=g0e[:, j, b : b + 1],
                in1=dn[b][:, j, :],
                op0=ALU.subtract,
                op1=ALU.mult,
            )

        def y_act(b, j):
            nc.scalar.activation(
                out=qq[b][:, j, :],
                in_=qq[b][:, j, :],
                func=AF.Identity,
                scale=0.5,
                bias=g0h[:, j, b : b + 1],
            )

        def y_on(b, j, eng):
            eng.tensor_scalar(
                out=qq[b][:, j, :],
                in0=qq[b][:, j, :],
                scalar1=half[:, 0:1],
                scalar2=g0h[:, j, b : b + 1],
                op0=ALU.mult,
                op1=ALU.add,
            )

        hg = {}
        hc = {}
        hs = {}

        def gate(b, h, nh):
            if h == 0:
                hg[b] = work.tile([P, T, J], BF16, name="hg", tag="hg", bufs=2, align_bytes=64)
            n = T // nh
            nc.vector.scalar_tensor_tensor(
                out=hg[b][:, h * n : (h + 1) * n, :],
                in0=th[b][:, :, h * n : (h + 1) * n].rearrange("p j t -> p t j"),
                scalar=1.0,
                in1=qq[b][:, :, h * n : (h + 1) * n].rearrange("p j t -> p t j"),
                op0=ALU.add,
                op1=ALU.mult,
            )

        def quant_h(b, h, nh):
            if h == 0:
                hc[b] = work.tile([P, T], U32, name="hc", tag="hc", bufs=2, align_bytes=64)
                hs[b] = work.tile([P, T], U8, name="hs", tag="hs", bufs=2, align_bytes=64)
            n = T // nh
            nc.vector.quantize_mx(
                out=hc[b][:, h * n : (h + 1) * n].bitcast(FP8X4),
                scales=hs[b][:, h * n : (h + 1) * n],
                in_=hg[b][:, h * n : (h + 1) * n, :].rearrange("p w t -> p (w t)"),
            )

        po = {}
        ost = {}

        def s2_mm(b, i):
            po[(b, i)] = bank([P, C], F32, "po")
            nc.tensor.matmul_mx(
                out=po[(b, i)][:],
                lhsT=hc[b][:, i * P : (i + 1) * P].bitcast(FP8X4),
                lhsT_scale=hs[b][:, i * P : (i + 1) * P],
                rhs=wc["o"][:].bitcast(FP8X4),
                rhs_scale=ws["o"][:],
                start=True,
                stop=True,
            )

        def ao(b, i, on_vector):
            if i == 0:
                ost[b] = work.tile([P, 4, C], F32, name="ost", tag="ost", bufs=3)
            if on_vector:
                nc.vector.tensor_copy(out=ost[b][:, i, :], in_=po[(b, i)][:])
            else:
                nc.scalar.copy(out=ost[b][:, i, :], in_=po[(b, i)][:])

        def store(b, h, nh):
            n = 4 // nh
            nc.sync.dma_start(
                out=out[b, h * n * P : (h + 1) * n * P, :].rearrange("(i p) c -> p i c", p=P),
                in_=ost[b][:, h * n : (h + 1) * n, :],
            )

        pta = bank([P, J, P], BF16, "pta")
        for j in range(J):
            nc.tensor.transpose(out=pta[:, j, :], in_=prma[:, j:C:J], identity=ident[:])
        pfa = const.tile([P, J, 4], F32)
        nc.vector.tensor_copy(out=pfa[:], in_=pta[:, :, 0:4])
        xpT = const.tile([P, J, B], BF16)
        nc.vector.tensor_copy(out=xpT[:], in_=pta[:, :, 24:32])
        transposes(0, (0,))
        make_dd(0, 0)
        make_dd(0, 1)
        transposes(0, (1,))
        make_dd(0, 2)
        make_dd(0, 3)
        pad_xT(0)
        evac_xT(0)
        dtab = const.tile([P, J, T], F32)
        beta = const.tile([P, J, B], F32)

        pfb = const.tile([P, J, 24], F32)
        negw = const.tile([P, J], F32)
        rb0 = const.tile([P, J, B], F32)
        g0 = const.tile([P, J, B], F32)
        et = const.tile([P, J, B], F32)
        g0e = const.tile([P, J, B], F32)
        g0h = const.tile([P, J, B], F32)
        lnb = const.tile([P, J, B], F32)

        def params_pe():
            ptb = bank([P, J, P], BF16, "ptb")
            for j in range(J):
                nc.tensor.transpose(out=ptb[:, j, :], in_=prmb[:, j:C:J], identity=ident[:])
            return ptb

        def params(ptb):
            nc.vector.tensor_copy(out=pfb[:], in_=ptb[:, :, 0:24])
            nc.vector.tensor_scalar(out=negw[:], in0=pfb[:, :, 0], scalar1=-1.0, scalar2=None, op0=ALU.mult)
            nc.vector.reciprocal(out=rb0[:], in_=pfb[:, :, 16:24])
            nc.vector.tensor_tensor(out=g0[:], in0=pfb[:, :, 8:16], in1=rb0[:], op=ALU.mult)
            nc.vector.tensor_scalar(out=et[:], in0=rb0[:], scalar1=EPS, scalar2=None, op0=ALU.mult)
            nc.vector.tensor_tensor(out=g0e[:], in0=g0[:], in1=et[:], op=ALU.mult)
            nc.vector.tensor_scalar(out=g0h[:], in0=g0[:], scalar1=0.5, scalar2=None, op0=ALU.mult)
            nc.scalar.activation(out=lnb[:], in_=pfb[:, :, 16:24], func=AF.Ln)

        LNS = {1: (0,), 3: (1, 2), 5: (3, 4), 7: (5, 6)}
        RG = (0,) * 8
        EVAC_V = ()
        AO_V = ()
        LIGHT = (2, 4, 6)
        SCALAR_R = (2, 4, 6)
        SCALAR_V = (4,)
        Y_VECTOR = ()
        ORDER0 = [(mi, j) for jh in (0, 2) for mi in (1, 0, 2) for j in (jh, jh + 1)]
        ORDER = [(mi, j) for mi in (1, 0, 2) for j in range(J)]
        for m in range(B):
            has_n = m + 1 < B
            h1 = m >= 1
            h3 = m >= 3
            lns = LNS.get(m, ())
            if h1 and m + 2 < B:
                load_x(m + 2, nc.sync)
            if has_n:
                pad_xT(m + 1)
            if h3 and m in Y_VECTOR:
                for j in range(J):
                    y_on(m - 3, j, nc.vector)
            if h1:
                alloc_b(m - 1)
                for j in range(J):
                    s1_mm(m - 1, j, "k")
                for j in range(J):
                    e_exp(m - 1, j)
                    if m == 1:
                        nc.scalar.activation(
                            out=dtab[:, j, :], in_=it_f[:], func=AF.Exp, scale=negw[:, j : j + 1]
                        )
                    if m not in LIGHT:
                        den(m - 1, j, nc.gpsimd)
                    s1_mm(m - 1, j, "r")
                for j in range(J):
                    e_tanh(m - 1, j)
                    s1_mm(m - 1, j, "v")
            if h3 and m not in Y_VECTOR:
                for j in range(J):
                    y_act(m - 3, j)
            qd = 0
            for s in range(13):
                while h1 and qd < J and (12, 12, 12, 12)[qd] <= s:
                    d_q(m - 1, qd)
                    qd += 1
                if s < 12:
                    mi, j = (ORDER if h1 else ORDER0)[s]
                    mix(m, j, mi)
                    if h1 and s >= 8 and has_n:
                        make_dd(m + 1, j)
                    if s == (3 if h1 else 7):
                        regroup_part("k", 0, T, "gpsimd")
                        if m in LIGHT:
                            for j2 in range(J):
                                den(m - 1, j2, nc.gpsimd)
                    if s == 7 and h1 and RG[m] > 0:
                        regroup_part("r", 0, RG[m], "gpsimd")
                if m == 0 and s == 2:
                    ptb = params_pe()
                    prep_w("k")
                if m == 0 and s == 5:
                    params(ptb)
                    transposes(1, (0, 1))
                    evac_xT(1)
                    prep_w("r")
                if m == 0 and s == 8:
                    prep_w("v")
            if m == 0:
                for j in range(J):
                    make_dd(1, j)
            if m in SCALAR_R:
                regroup_part("r", RG[m], T, "scalar")
            for b in lns:
                for j in range(J):
                    a_ln(b, j)
            if m == 1:
                prep_w("o")
            if m in SCALAR_V:
                regroup_part("v", 0, T, "scalar")
            if h1 and has_n:
                transposes(m + 1, (0, 1))
                evac_xT(m + 1, m in EVAC_V)
            for b in lns:
                a_rho(b)
            if 4 <= m < B - 1:
                for i in range(4):
                    s2_mm(m - 4, i)
                    ao(m - 4, i, m in AO_V and i % 2 == 1)
                store(m - 4, 0, 1)
            if m == 0:
                nc.vector.tensor_tensor(
                    out=beta[:], in0=pfb[:, :, 1:2].to_broadcast([P, J, B]), in1=lnb[:], op=ALU.subtract
                )
            if m not in SCALAR_R:
                regroup_part("r", RG[m], T, "vector")
            if m not in SCALAR_V:
                regroup_part("v", 0, T, "vector")
            if m == 0:
                quant_w("k")
            quant_x(m, "k")
            if h3:
                gate(m - 3, 0, 1)
            if m == 0:
                quant_w("r")
            quant_x(m, "r")
            if m == 0:
                quant_w("v")
            if m == 1:
                quant_w("o")
            quant_x(m, "v")
            if m >= 2:
                for j in range(J):
                    d_x(m - 2, j)
            if h3:
                quant_h(m - 3, 0, 1)

        l7 = B - 1
        l6 = B - 2
        l5 = B - 3
        l4 = B - 4
        alloc_b(l7)
        for j in range(J):
            s1_mm(l7, j, "k")
        for j in range(J):
            e_exp(l7, j)
            den(l7, j, nc.vector)
            s1_mm(l7, j, "v")
        for i in range(4):
            s2_mm(B - 5, i)
            ao(B - 5, i, False)
        store(B - 5, 0, 1)
        for j in range(J):
            d_x(l6, j)
        for j in range(J):
            y_on(l5, j, nc.vector)
        for j in range(J):
            d_q(l7, j)
        for j in range(J):
            a_ln(l7, j)
        gate(l5, 0, 1)
        quant_h(l5, 0, 1)
        for j in range(J):
            y_on(l6, j, nc.vector)
        for j in range(J):
            a_rhoj(l7, j)
        for j in range(J):
            s1_mm(l7, j, "r")
        for j in range(J):
            e_tanh(l7, j)
        for i in range(4):
            s2_mm(l4, i)
            ao(l4, i, False)
            if i % 2 == 1:
                store(l4, i // 2, 2)
        for j in range(J):
            d_x(l7, j)
        for j in range(J):
            y_act(l7, j)
        gate(l6, 0, 1)
        quant_h(l6, 0, 1)
        for i in range(4):
            s2_mm(l5, i)
            ao(l5, i, False)
            if i % 2 == 1:
                store(l5, i // 2, 2)
        for h in range(NH):
            gate(l7, h, NH)
            if h > 0:
                quant_h(l7, h - 1, NH)
        quant_h(l7, NH - 1, NH)
        for i in range(4):
            s2_mm(l6, i)
            ao(l6, i, False)
            if i % 2 == 1:
                store(l6, i // 2, 2)
        for h in range(NH):
            for i in range(h * 4 // NH, (h + 1) * 4 // NH):
                s2_mm(l7, i)
                ao(l7, i, i % 2 == 1)
            store(l7, h, NH)
